import numpy as np
import ml_dtypes


def mxq(x, axis, fmt="e4m3"):
    dtype, down = {"e4m3": (ml_dtypes.float8_e4m3fn, 7), "e5m2": (ml_dtypes.float8_e5m2, 14)}[fmt]
    v = np.moveaxis(np.asarray(x, np.float32).astype(ml_dtypes.bfloat16).astype(np.float64), axis, -1)
    blocks = v.reshape(v.shape[:-1] + (-1, 32))
    amax = np.abs(blocks).max(-1, keepdims=True)
    byte = np.maximum(np.where(amax > 0, np.frexp(amax)[1] - 1 + 127, 0) - down, 1)
    scale = np.exp2(byte - 127.0)
    codes = (blocks / scale).astype(np.float32).astype(dtype).astype(np.float64)
    return np.moveaxis((codes * scale).reshape(v.shape), -1, axis)


WIDE = False


def mx_kscale(k):
    if not WIDE:
        return np.ones(k)
    levels = np.array([10, -10, 5, -5, 0])
    a = np.random.permutation(np.resize(levels, k // 512 * 4)).reshape(k // 512, 4)
    idx = np.arange(k)
    return np.exp2(a[idx // 512, idx % 128 // 32])


BF16 = ml_dtypes.bfloat16


def bf(x):
    return np.asarray(x, np.float32).astype(BF16)


def f64(x):
    return np.asarray(x).astype(np.float64)


B, S, D, E = 2, 512, 512, 128


def setup_inputs():
    s, t = mx_kscale(S), mx_kscale(D)
    return {"q": bf(np.random.standard_normal((B, S, D)) / t),
            "k": bf(np.random.standard_normal((B, S, D)) * s[:, None] * t),
            "v": bf(np.random.standard_normal((B, S, E)) / s[:, None])}


def reference(q, k, v):
    scale = 1.0 / np.sqrt(q.shape[1])
    qn = f64(q) * scale
    kn = f64(k) * scale
    kv_mat = mxq(kn, 1, "e4m3").transpose(0, 2, 1) @ mxq(f64(v), 1, "e4m3")
    out = mxq(qn, 2, "e4m3") @ mxq(kv_mat, 1, "e4m3")
    return out

@@ -1,0 +1,166 @@
+import math
+from contextlib import ExitStack
+
+import concourse.mybir as mybir
+from concourse.masks import make_identity
+
+BF16 = mybir.dt.bfloat16
+F32 = mybir.dt.float32
+U32 = mybir.dt.uint32
+U8 = mybir.dt.uint8
+FP8X4 = mybir.dt.float8_e4m3fn_x4
+
+B, S, D, E = 2, 512, 512, 128
+P = 128
+PACK = 4
+PAIRS = D // 2
+HALVES = 2
+ROWS = 2
+
+FLOPS = 2 * 2 * B * S * D * E
+SCALE = 1.0 / math.sqrt(S)
+
+K_PAIRS_ON_VECTOR = 168
+
+
+def tile_efficientattention_s_kernel(tc, q, k, v, out):
+    nc = tc.nc
+    with ExitStack() as ctx:
+        keep = ctx.enter_context(tc.tile_pool(name="keep", bufs=1))
+        qt_banks = ctx.enter_context(tc.psum_pool(name="qt_banks", bufs=4))
+        kv_banks = ctx.enter_context(tc.psum_pool(name="kv_banks", bufs=2))
+        out_banks = ctx.enter_context(tc.psum_pool(name="out_banks", bufs=2))
+
+        v_raw = keep.tile([P, B, PACK, E], BF16)
+        nc.sync.dma_start(out=v_raw[:], in_=v.rearrange("b (p j) e -> p b j e", j=PACK))
+        k_raw = []
+        for b in range(B):
+            k_raw_b = keep.tile([P, PACK, D], BF16, name="k_raw%d" % b)
+            nc.sync.dma_start(out=k_raw_b[:], in_=k[b].rearrange("(p j) d -> p j d", j=PACK))
+            k_raw.append(k_raw_b)
+        q_raw = {}
+        for b in range(B):
+            for h in range(HALVES):
+                rows = slice(h * ROWS * P, (h + 1) * ROWS * P)
+                q_raw_bh = keep.tile([P, ROWS, D], BF16, name="q_raw%d%d" % (b, h))
+                nc.sync.dma_start(
+                    out=q_raw_bh[:], in_=q[b, rows, :].rearrange("(p r) d -> p r d", r=ROWS)
+                )
+                q_raw[(b, h)] = q_raw_bh
+
+        identity = keep.tile([P, P], F32)
+        make_identity(nc, identity[:])
+
+        v_grouped = keep.tile([P, B, E, PACK], BF16, align_bytes=64)
+        v_codes = keep.tile([P, B * E], U32, align_bytes=64)
+        v_scales = keep.tile([P, B * E], U8, align_bytes=64)
+        nc.vector.tensor_copy(out=v_grouped[:], in_=v_raw[:].rearrange("p b j e -> p b e j"))
+        nc.vector.quantize_mx(
+            out=v_codes[:].bitcast(FP8X4),
+            scales=v_scales[:],
+            in_=v_grouped[:].rearrange("p b e j -> p (b e j)"),
+        )
+
+        kv_codes = []
+        kv_scales = []
+        for b in range(B):
+            k_grouped = keep.tile([P, D, PACK], BF16, name="k_grouped%d" % b, align_bytes=64)
+            k_source = k_raw[b][:].rearrange("p j (w e) -> p w j e", e=2)
+            k_target = k_grouped[:].rearrange("p (e w) j -> p w j e", e=2)
+            split = K_PAIRS_ON_VECTOR
+            nc.vector.tensor_scalar_mul(
+                out=k_target[:, :split], in0=k_source[:, :split], scalar1=SCALE
+            )
+            nc.scalar.mul(out=k_target[:, split:], in_=k_source[:, split:], mul=SCALE)
+
+            k_codes = keep.tile([P, D], U32, name="k_codes%d" % b, align_bytes=64)
+            k_scales = keep.tile([P, D], U8, name="k_scales%d" % b, align_bytes=64)
+            nc.vector.quantize_mx(
+                out=k_codes[:].bitcast(FP8X4),
+                scales=k_scales[:],
+                in_=k_grouped[:].rearrange("p c j -> p (c j)"),
+            )
+
+            kv_psum = kv_banks.tile([P, PACK, E], F32, name="kv_psum")
+            value_cols = slice(b * E, (b + 1) * E)
+            for i in range(PACK):
+                feature_cols = slice(i * P, (i + 1) * P)
+                nc.tensor.matmul_mx(
+                    out=kv_psum[:, i, :],
+                    lhsT=k_codes[:, feature_cols].bitcast(FP8X4),
+                    lhsT_scale=k_scales[:, feature_cols],
+                    rhs=v_codes[:, value_cols].bitcast(FP8X4),
+                    rhs_scale=v_scales[:, value_cols],
+                    start=True,
+                    stop=True,
+                )
+
+            kv_grouped = keep.tile([P, E, PACK], BF16, name="kv_grouped%d" % b, align_bytes=64)
+            nc.scalar.copy(
+                out=kv_grouped[:].rearrange("p n (u e) -> p n u e", e=2),
+                in_=kv_psum[:].rearrange("p (e u) n -> p n u e", e=2),
+            )
+            kv_codes_b = keep.tile([P, E], U32, name="kv_codes%d" % b, align_bytes=64)
+            kv_scales_b = keep.tile([P, E], U8, name="kv_scales%d" % b, align_bytes=64)
+            nc.vector.quantize_mx(
+                out=kv_codes_b[:].bitcast(FP8X4),
+                scales=kv_scales_b[:],
+                in_=kv_grouped[:].rearrange("p n t -> p (n t)"),
+            )
+            kv_codes.append(kv_codes_b)
+            kv_scales.append(kv_scales_b)
+
+        for b in range(B):
+            for h in range(HALVES):
+                q_words = q_raw[(b, h)][:].rearrange("p r d -> p (r d)").bitcast(F32)
+                qt_psum = qt_banks.tile([P, 2 * ROWS * P], F32, name="qt_psum")
+                for u in range(2):
+                    for r in range(ROWS):
+                        block = u * ROWS + r
+                        first_word = r * PAIRS + u * P
+                        nc.tensor.transpose(
+                            qt_psum[:, block * P : (block + 1) * P],
+                            q_words[:, first_word : first_word + P],
+                            identity[:],
+                        )
+
+                q_grouped = keep.tile(
+                    [P, ROWS * P, PACK], BF16, name="q_grouped%d%d" % (b, h), align_bytes=64
+                )
+                q_source = qt_psum[:].bitcast(BF16).rearrange("p (u m e) -> p m u e", u=2, e=2)
+                q_target = q_grouped[:].rearrange("p m (u e) -> p m u e", e=2)
+                if h % 2 == 0:
+                    nc.scalar.mul(out=q_target, in_=q_source, mul=SCALE)
+                else:
+                    nc.vector.tensor_scalar_mul(out=q_target, in0=q_source, scalar1=SCALE)
+
+                q_codes = keep.tile([P, ROWS * P], U32, name="q_codes%d%d" % (b, h), align_bytes=64)
+                q_scales = keep.tile([P, ROWS * P], U8, name="q_scales%d%d" % (b, h), align_bytes=64)
+                nc.vector.quantize_mx(
+                    out=q_codes[:].bitcast(FP8X4),
+                    scales=q_scales[:],
+                    in_=q_grouped[:].rearrange("p m t -> p (m t)"),
+                )
+
+                out_psum = out_banks.tile([P, ROWS, E], F32, name="out_psum")
+                for r in range(ROWS):
+                    row_cols = slice(r * P, (r + 1) * P)
+                    nc.tensor.matmul_mx(
+                        out=out_psum[:, r, :],
+                        lhsT=q_codes[:, row_cols].bitcast(FP8X4),
+                        lhsT_scale=q_scales[:, row_cols],
+                        rhs=kv_codes[b][:].bitcast(FP8X4),
+                        rhs_scale=kv_scales[b][:],
+                        start=True,
+                        stop=True,
+                    )
+
+                out_sbuf = keep.tile([P, ROWS, E], F32, name="out_sbuf%d%d" % (b, h))
+                if h % 2 == 0:
+                    nc.scalar.copy(out=out_sbuf[:], in_=out_psum[:])
+                else:
+                    nc.vector.tensor_copy(out=out_sbuf[:], in_=out_psum[:])
+                rows = slice(h * ROWS * P, (h + 1) * ROWS * P)
+                nc.sync.dma_start(
+                    out=out[b, rows, :].rearrange("(p r) e -> p r e", r=ROWS), in_=out_sbuf[:]
+                )

@@ -27,26 +27,25 @@ def tile_efficientattention_s_kernel(tc, q, k, v, out):
     nc = tc.nc
     with ExitStack() as ctx:
         keep = ctx.enter_context(tc.tile_pool(name="keep", bufs=1))
-        qt_banks = ctx.enter_context(tc.psum_pool(name="qt_banks", bufs=4))
-        kv_banks = ctx.enter_context(tc.psum_pool(name="kv_banks", bufs=2))
+        qt_banks = ctx.enter_context(tc.psum_pool(name="qt_banks", bufs=B * HALVES))
+        kv_banks = ctx.enter_context(tc.psum_pool(name="kv_banks", bufs=B))
         out_banks = ctx.enter_context(tc.psum_pool(name="out_banks", bufs=2))
+        ctx.enter_context(tc.manual_schedule())
 
         v_raw = keep.tile([P, B, PACK, E], BF16)
         nc.sync.dma_start(out=v_raw[:], in_=v.rearrange("b (p j) e -> p b j e", j=PACK))
-        k_raw = []
-        for b in range(B):
-            k_raw_b = keep.tile([P, PACK, D], BF16, name="k_raw%d" % b)
-            nc.sync.dma_start(out=k_raw_b[:], in_=k[b].rearrange("(p j) d -> p j d", j=PACK))
-            k_raw.append(k_raw_b)
+        k_raw = {}
         q_raw = {}
         for b in range(B):
+            k_raw[b] = keep.tile([P, PACK, D], BF16, name="k_raw%d" % b)
+            nc.sync.dma_start(out=k_raw[b][:], in_=k[b].rearrange("(p j) d -> p j d", j=PACK))
             for h in range(HALVES):
                 rows = slice(h * ROWS * P, (h + 1) * ROWS * P)
-                q_raw_bh = keep.tile([P, ROWS, D], BF16, name="q_raw%d%d" % (b, h))
+                q_raw[(b, h)] = keep.tile([P, ROWS, D], BF16, name="q_raw%d%d" % (b, h))
                 nc.sync.dma_start(
-                    out=q_raw_bh[:], in_=q[b, rows, :].rearrange("(p r) d -> p r d", r=ROWS)
+                    out=q_raw[(b, h)][:],
+                    in_=q[b, rows, :].rearrange("(p r) d -> p r d", r=ROWS),
                 )
-                q_raw[(b, h)] = q_raw_bh
 
         identity = keep.tile([P, P], F32)
         make_identity(nc, identity[:])
@@ -61,17 +60,31 @@ def tile_efficientattention_s_kernel(tc, q, k, v, out):
             in_=v_grouped[:].rearrange("p b e j -> p (b e j)"),
         )
 
-        kv_codes = []
-        kv_scales = []
+        qt_psum = {}
+        kv_psum = {}
         for b in range(B):
+            for h in range(HALVES):
+                q_words = q_raw[(b, h)][:].rearrange("p r d -> p (r d)").bitcast(F32)
+                qt_psum[(b, h)] = qt_banks.tile([P, 2 * ROWS * P], F32, name="qt_psum")
+                for u in range(2):
+                    for r in range(ROWS):
+                        block = u * ROWS + r
+                        first_word = r * PAIRS + u * P
+                        nc.tensor.transpose(
+                            qt_psum[(b, h)][:, block * P : (block + 1) * P],
+                            q_words[:, first_word : first_word + P],
+                            identity[:],
+                        )
+
             k_grouped = keep.tile([P, D, PACK], BF16, name="k_grouped%d" % b, align_bytes=64)
             k_source = k_raw[b][:].rearrange("p j (w e) -> p w j e", e=2)
             k_target = k_grouped[:].rearrange("p (e w) j -> p w j e", e=2)
-            split = K_PAIRS_ON_VECTOR
+            split = K_PAIRS_ON_VECTOR if b == 0 else PAIRS
             nc.vector.tensor_scalar_mul(
                 out=k_target[:, :split], in0=k_source[:, :split], scalar1=SCALE
             )
-            nc.scalar.mul(out=k_target[:, split:], in_=k_source[:, split:], mul=SCALE)
+            if split < PAIRS:
+                nc.scalar.mul(out=k_target[:, split:], in_=k_source[:, split:], mul=SCALE)
 
             k_codes = keep.tile([P, D], U32, name="k_codes%d" % b, align_bytes=64)
             k_scales = keep.tile([P, D], U8, name="k_scales%d" % b, align_bytes=64)
@@ -81,12 +94,12 @@ def tile_efficientattention_s_kernel(tc, q, k, v, out):
                 in_=k_grouped[:].rearrange("p c j -> p (c j)"),
             )
 
-            kv_psum = kv_banks.tile([P, PACK, E], F32, name="kv_psum")
+            kv_psum[b] = kv_banks.tile([P, PACK, E], F32, name="kv_psum")
             value_cols = slice(b * E, (b + 1) * E)
             for i in range(PACK):
                 feature_cols = slice(i * P, (i + 1) * P)
                 nc.tensor.matmul_mx(
-                    out=kv_psum[:, i, :],
+                    out=kv_psum[b][:, i, :],
                     lhsT=k_codes[:, feature_cols].bitcast(FP8X4),
                     lhsT_scale=k_scales[:, feature_cols],
                     rhs=v_codes[:, value_cols].bitcast(FP8X4),
@@ -95,66 +108,65 @@ def tile_efficientattention_s_kernel(tc, q, k, v, out):
                     stop=True,
                 )
 
+        q_codes = {}
+        q_scales = {}
+        kv_codes = {}
+        kv_scales = {}
+        for b in range(B):
+            q_grouped = {}
+            for h in range(HALVES):
+                q_grouped[h] = keep.tile(
+                    [P, ROWS * P, PACK], BF16, name="q_grouped%d%d" % (b, h), align_bytes=64
+                )
+                q_source = (
+                    qt_psum[(b, h)][:].bitcast(BF16).rearrange("p (u m e) -> p m u e", u=2, e=2)
+                )
+                q_target = q_grouped[h][:].rearrange("p m (u e) -> p m u e", e=2)
+                if (b, h) == (B - 1, HALVES - 1):
+                    nc.vector.tensor_scalar_mul(out=q_target, in0=q_source, scalar1=SCALE)
+                else:
+                    nc.scalar.mul(out=q_target, in_=q_source, mul=SCALE)
+
             kv_grouped = keep.tile([P, E, PACK], BF16, name="kv_grouped%d" % b, align_bytes=64)
             nc.scalar.copy(
                 out=kv_grouped[:].rearrange("p n (u e) -> p n u e", e=2),
-                in_=kv_psum[:].rearrange("p (e u) n -> p n u e", e=2),
+                in_=kv_psum[b][:].rearrange("p (e u) n -> p n u e", e=2),
             )
-            kv_codes_b = keep.tile([P, E], U32, name="kv_codes%d" % b, align_bytes=64)
-            kv_scales_b = keep.tile([P, E], U8, name="kv_scales%d" % b, align_bytes=64)
+
+            for h in range(HALVES):
+                q_codes[(b, h)] = keep.tile(
+                    [P, ROWS * P], U32, name="q_codes%d%d" % (b, h), align_bytes=64
+                )
+                q_scales[(b, h)] = keep.tile(
+                    [P, ROWS * P], U8, name="q_scales%d%d" % (b, h), align_bytes=64
+                )
+                nc.vector.quantize_mx(
+                    out=q_codes[(b, h)][:].bitcast(FP8X4),
+                    scales=q_scales[(b, h)][:],
+                    in_=q_grouped[h][:].rearrange("p m t -> p (m t)"),
+                )
+            kv_codes[b] = keep.tile([P, E], U32, name="kv_codes%d" % b, align_bytes=64)
+            kv_scales[b] = keep.tile([P, E], U8, name="kv_scales%d" % b, align_bytes=64)
             nc.vector.quantize_mx(
-                out=kv_codes_b[:].bitcast(FP8X4),
-                scales=kv_scales_b[:],
+                out=kv_codes[b][:].bitcast(FP8X4),
+                scales=kv_scales[b][:],
                 in_=kv_grouped[:].rearrange("p n t -> p (n t)"),
             )
-            kv_codes.append(kv_codes_b)
-            kv_scales.append(kv_scales_b)
 
         for b in range(B):
             for h in range(HALVES):
-                q_words = q_raw[(b, h)][:].rearrange("p r d -> p (r d)").bitcast(F32)
-                qt_psum = qt_banks.tile([P, 2 * ROWS * P], F32, name="qt_psum")
-                for u in range(2):
-                    for r in range(ROWS):
-                        block = u * ROWS + r
-                        first_word = r * PAIRS + u * P
-                        nc.tensor.transpose(
-                            qt_psum[:, block * P : (block + 1) * P],
-                            q_words[:, first_word : first_word + P],
-                            identity[:],
-                        )
-
-                q_grouped = keep.tile(
-                    [P, ROWS * P, PACK], BF16, name="q_grouped%d%d" % (b, h), align_bytes=64
-                )
-                q_source = qt_psum[:].bitcast(BF16).rearrange("p (u m e) -> p m u e", u=2, e=2)
-                q_target = q_grouped[:].rearrange("p m (u e) -> p m u e", e=2)
-                if h % 2 == 0:
-                    nc.scalar.mul(out=q_target, in_=q_source, mul=SCALE)
-                else:
-                    nc.vector.tensor_scalar_mul(out=q_target, in0=q_source, scalar1=SCALE)
-
-                q_codes = keep.tile([P, ROWS * P], U32, name="q_codes%d%d" % (b, h), align_bytes=64)
-                q_scales = keep.tile([P, ROWS * P], U8, name="q_scales%d%d" % (b, h), align_bytes=64)
-                nc.vector.quantize_mx(
-                    out=q_codes[:].bitcast(FP8X4),
-                    scales=q_scales[:],
-                    in_=q_grouped[:].rearrange("p m t -> p (m t)"),
-                )
-
                 out_psum = out_banks.tile([P, ROWS, E], F32, name="out_psum")
                 for r in range(ROWS):
                     row_cols = slice(r * P, (r + 1) * P)
                     nc.tensor.matmul_mx(
                         out=out_psum[:, r, :],
-                        lhsT=q_codes[:, row_cols].bitcast(FP8X4),
-                        lhsT_scale=q_scales[:, row_cols],
+                        lhsT=q_codes[(b, h)][:, row_cols].bitcast(FP8X4),
+                        lhsT_scale=q_scales[(b, h)][:, row_cols],
                         rhs=kv_codes[b][:].bitcast(FP8X4),
                         rhs_scale=kv_scales[b][:],
                         start=True,
                         stop=True,
                     )
-
                 out_sbuf = keep.tile([P, ROWS, E], F32, name="out_sbuf%d%d" % (b, h))
                 if h % 2 == 0:
                     nc.scalar.copy(out=out_sbuf[:], in_=out_psum[:])

import math
from contextlib import ExitStack

import concourse.mybir as mybir
from concourse.masks import make_identity

BF16 = mybir.dt.bfloat16
F32 = mybir.dt.float32
U32 = mybir.dt.uint32
U8 = mybir.dt.uint8
FP8X4 = mybir.dt.float8_e4m3fn_x4

B, S, D, E = 2, 512, 512, 128
P = 128
PACK = 4
PAIRS = D // 2
HALVES = 2
ROWS = 2

FLOPS = 2 * 2 * B * S * D * E
SCALE = 1.0 / math.sqrt(S)

K_PAIRS_ON_VECTOR = 168


def tile_efficientattention_s_kernel(tc, q, k, v, out):
    nc = tc.nc
    with ExitStack() as ctx:
        keep = ctx.enter_context(tc.tile_pool(name="keep", bufs=1))
        qt_banks = ctx.enter_context(tc.psum_pool(name="qt_banks", bufs=B * HALVES))
        kv_banks = ctx.enter_context(tc.psum_pool(name="kv_banks", bufs=B))
        out_banks = ctx.enter_context(tc.psum_pool(name="out_banks", bufs=2))
        ctx.enter_context(tc.manual_schedule())

        v_raw = keep.tile([P, B, PACK, E], BF16)
        nc.sync.dma_start(out=v_raw[:], in_=v.rearrange("b (p j) e -> p b j e", j=PACK))
        k_raw = {}
        q_raw = {}
        for b in range(B):
            k_raw[b] = keep.tile([P, PACK, D], BF16, name="k_raw%d" % b)
            nc.sync.dma_start(out=k_raw[b][:], in_=k[b].rearrange("(p j) d -> p j d", j=PACK))
            for h in range(HALVES):
                rows = slice(h * ROWS * P, (h + 1) * ROWS * P)
                q_raw[(b, h)] = keep.tile([P, ROWS, D], BF16, name="q_raw%d%d" % (b, h))
                nc.sync.dma_start(
                    out=q_raw[(b, h)][:],
                    in_=q[b, rows, :].rearrange("(p r) d -> p r d", r=ROWS),
                )

        identity = keep.tile([P, P], F32)
        make_identity(nc, identity[:])

        v_grouped = keep.tile([P, B, E, PACK], BF16, align_bytes=64)
        v_codes = keep.tile([P, B * E], U32, align_bytes=64)
        v_scales = keep.tile([P, B * E], U8, align_bytes=64)
        nc.vector.tensor_copy(out=v_grouped[:], in_=v_raw[:].rearrange("p b j e -> p b e j"))
        nc.vector.quantize_mx(
            out=v_codes[:].bitcast(FP8X4),
            scales=v_scales[:],
            in_=v_grouped[:].rearrange("p b e j -> p (b e j)"),
        )

        qt_psum = {}
        kv_psum = {}
        for b in range(B):
            for h in range(HALVES):
                q_words = q_raw[(b, h)][:].rearrange("p r d -> p (r d)").bitcast(F32)
                qt_psum[(b, h)] = qt_banks.tile([P, 2 * ROWS * P], F32, name="qt_psum")
                for u in range(2):
                    for r in range(ROWS):
                        block = u * ROWS + r
                        first_word = r * PAIRS + u * P
                        nc.tensor.transpose(
                            qt_psum[(b, h)][:, block * P : (block + 1) * P],
                            q_words[:, first_word : first_word + P],
                            identity[:],
                        )

            k_grouped = keep.tile([P, D, PACK], BF16, name="k_grouped%d" % b, align_bytes=64)
            k_source = k_raw[b][:].rearrange("p j (w e) -> p w j e", e=2)
            k_target = k_grouped[:].rearrange("p (e w) j -> p w j e", e=2)
            split = K_PAIRS_ON_VECTOR if b == 0 else PAIRS
            nc.vector.tensor_scalar_mul(
                out=k_target[:, :split], in0=k_source[:, :split], scalar1=SCALE
            )
            if split < PAIRS:
                nc.scalar.mul(out=k_target[:, split:], in_=k_source[:, split:], mul=SCALE)

            k_codes = keep.tile([P, D], U32, name="k_codes%d" % b, align_bytes=64)
            k_scales = keep.tile([P, D], U8, name="k_scales%d" % b, align_bytes=64)
            nc.vector.quantize_mx(
                out=k_codes[:].bitcast(FP8X4),
                scales=k_scales[:],
                in_=k_grouped[:].rearrange("p c j -> p (c j)"),
            )

            kv_psum[b] = kv_banks.tile([P, PACK, E], F32, name="kv_psum")
            value_cols = slice(b * E, (b + 1) * E)
            for i in range(PACK):
                feature_cols = slice(i * P, (i + 1) * P)
                nc.tensor.matmul_mx(
                    out=kv_psum[b][:, i, :],
                    lhsT=k_codes[:, feature_cols].bitcast(FP8X4),
                    lhsT_scale=k_scales[:, feature_cols],
                    rhs=v_codes[:, value_cols].bitcast(FP8X4),
                    rhs_scale=v_scales[:, value_cols],
                    start=True,
                    stop=True,
                )

        q_codes = {}
        q_scales = {}
        kv_codes = {}
        kv_scales = {}
        for b in range(B):
            q_grouped = {}
            for h in range(HALVES):
                q_grouped[h] = keep.tile(
                    [P, ROWS * P, PACK], BF16, name="q_grouped%d%d" % (b, h), align_bytes=64
                )
                q_source = (
                    qt_psum[(b, h)][:].bitcast(BF16).rearrange("p (u m e) -> p m u e", u=2, e=2)
                )
                q_target = q_grouped[h][:].rearrange("p m (u e) -> p m u e", e=2)
                if (b, h) == (B - 1, HALVES - 1):
                    nc.vector.tensor_scalar_mul(out=q_target, in0=q_source, scalar1=SCALE)
                else:
                    nc.scalar.mul(out=q_target, in_=q_source, mul=SCALE)

            kv_grouped = keep.tile([P, E, PACK], BF16, name="kv_grouped%d" % b, align_bytes=64)
            nc.scalar.copy(
                out=kv_grouped[:].rearrange("p n (u e) -> p n u e", e=2),
                in_=kv_psum[b][:].rearrange("p (e u) n -> p n u e", e=2),
            )

            for h in range(HALVES):
                q_codes[(b, h)] = keep.tile(
                    [P, ROWS * P], U32, name="q_codes%d%d" % (b, h), align_bytes=64
                )
                q_scales[(b, h)] = keep.tile(
                    [P, ROWS * P], U8, name="q_scales%d%d" % (b, h), align_bytes=64
                )
                nc.vector.quantize_mx(
                    out=q_codes[(b, h)][:].bitcast(FP8X4),
                    scales=q_scales[(b, h)][:],
                    in_=q_grouped[h][:].rearrange("p m t -> p (m t)"),
                )
            kv_codes[b] = keep.tile([P, E], U32, name="kv_codes%d" % b, align_bytes=64)
            kv_scales[b] = keep.tile([P, E], U8, name="kv_scales%d" % b, align_bytes=64)
            nc.vector.quantize_mx(
                out=kv_codes[b][:].bitcast(FP8X4),
                scales=kv_scales[b][:],
                in_=kv_grouped[:].rearrange("p n t -> p (n t)"),
            )

        for b in range(B):
            for h in range(HALVES):
                out_psum = out_banks.tile([P, ROWS, E], F32, name="out_psum")
                for r in range(ROWS):
                    row_cols = slice(r * P, (r + 1) * P)
                    nc.tensor.matmul_mx(
                        out=out_psum[:, r, :],
                        lhsT=q_codes[(b, h)][:, row_cols].bitcast(FP8X4),
                        lhsT_scale=q_scales[(b, h)][:, row_cols],
                        rhs=kv_codes[b][:].bitcast(FP8X4),
                        rhs_scale=kv_scales[b][:],
                        start=True,
                        stop=True,
                    )
                out_sbuf = keep.tile([P, ROWS, E], F32, name="out_sbuf%d%d" % (b, h))
                if h % 2 == 0:
                    nc.scalar.copy(out=out_sbuf[:], in_=out_psum[:])
                else:
                    nc.vector.tensor_copy(out=out_sbuf[:], in_=out_psum[:])
                rows = slice(h * ROWS * P, (h + 1) * ROWS * P)
                nc.sync.dma_start(
                    out=out[b, rows, :].rearrange("(p r) e -> p r e", r=ROWS), in_=out_sbuf[:]
                )
